import numpy as np
import ml_dtypes


def mxq(x, axis, fmt="e4m3"):
    dtype, down = {"e4m3": (ml_dtypes.float8_e4m3fn, 7), "e5m2": (ml_dtypes.float8_e5m2, 14)}[fmt]
    v = np.moveaxis(np.asarray(x, np.float32).astype(ml_dtypes.bfloat16).astype(np.float64), axis, -1)
    blocks = v.reshape(v.shape[:-1] + (-1, 32))
    amax = np.abs(blocks).max(-1, keepdims=True)
    byte = np.maximum(np.where(amax > 0, np.frexp(amax)[1] - 1 + 127, 0) - down, 1)
    scale = np.exp2(byte - 127.0)
    codes = (blocks / scale).astype(np.float32).astype(dtype).astype(np.float64)
    return np.moveaxis((codes * scale).reshape(v.shape), -1, axis)


WIDE = False


def mx_kscale(k):
    if not WIDE:
        return np.ones(k)
    levels = np.array([10, -10, 5, -5, 0])
    a = np.random.permutation(np.resize(levels, k // 512 * 4)).reshape(k // 512, 4)
    idx = np.arange(k)
    return np.exp2(a[idx // 512, idx % 128 // 32])


BF16 = ml_dtypes.bfloat16


def bf(x):
    return np.asarray(x, np.float32).astype(BF16)


def f64(x):
    return np.asarray(x).astype(np.float64)


B, D, C, NP, NS = 4096, 1024, 512, 512, 512


def relu(v):
    return np.maximum(v, 0.0)


def setup_inputs():
    s = mx_kscale(D)
    t = mx_kscale(NS)
    return {
        "x_batch": bf(np.random.uniform(size=(B, D)) * s),
        "predicted": bf(np.random.standard_normal((B, D)) * s),
        "W_vip_td": bf(np.random.standard_normal((NS, D)) / np.sqrt(D) / s * t[:, None]),
        "W_som_in": bf(np.random.standard_normal((NS, D)) * 1.5 / np.sqrt(D) / s),
        "W_vip_som": bf(np.random.standard_normal((NS, NS)) / np.sqrt(NS) / t),
    }


def reference(x_batch, predicted, W_vip_td, W_som_in, W_vip_som):
    r_vip = relu(mxq(f64(predicted), 1, "e4m3") @ mxq(f64(W_vip_td), 1, "e4m3").T)
    som_ff = relu(mxq(f64(x_batch), 1, "e4m3") @ mxq(f64(W_som_in), 1, "e4m3").T)
    r_som = relu(som_ff - (mxq(r_vip, 1, "e4m3") @ mxq(f64(W_vip_som), 1, "e4m3").T))
    return r_som

@@ -1,0 +1,277 @@
+from contextlib import ExitStack
+
+import concourse.mybir as mybir
+from concourse.masks import make_identity
+
+F32 = mybir.dt.float32
+BF16 = mybir.dt.bfloat16
+U32 = mybir.dt.uint32
+U8 = mybir.dt.uint8
+FP8X4 = mybir.dt.float8_e4m3fn_x4
+RELU = mybir.ActivationFunctionType.Relu
+SUBTRACT = mybir.AluOpType.subtract
+
+BATCH = 4096
+D_IN = 1024
+CELLS = 512
+FLOPS = 2 * BATCH * CELLS * (2 * D_IN + CELLS)
+
+P = 128
+PACK = 4
+K_PASS = P * PACK
+D_PASSES = D_IN // K_PASS
+BANK = 512
+BLOCKS = BANK // P
+
+TILES = BATCH // P
+CHUNK_TILES = 2
+CHUNKS = TILES // CHUNK_TILES
+ROUND_CHUNKS = 1
+ROUND_TILES = ROUND_CHUNKS * CHUNK_TILES
+UNITS = CHUNKS // ROUND_CHUNKS
+X_LAG = 2
+LOAD_AHEAD = 3
+VECTOR_SHARE = 4
+
+
+def tile_pecircuits_pa_t_kernel(
+    tc, x_batch, predicted, W_vip_td, W_som_in, W_vip_som, out
+):
+    nc = tc.nc
+
+    pred_chunks = predicted.rearrange("(c p t) k -> c p (t k)", p=P, t=CHUNK_TILES)
+    x_chunks = x_batch.rearrange("(c p t) k -> c p (t k)", p=P, t=CHUNK_TILES)
+    out_chunks = out.rearrange("(c p t) n -> c p (t n)", p=P, t=CHUNK_TILES)
+
+    with ExitStack() as stack:
+        const = stack.enter_context(tc.tile_pool(name="const", bufs=1))
+        raw_pool = stack.enter_context(
+            tc.tile_pool(name="raw", bufs=(LOAD_AHEAD + 1) * ROUND_CHUNKS)
+        )
+        grouped_pool = stack.enter_context(tc.tile_pool(name="grouped", bufs=4 * ROUND_TILES))
+        codes_pool = stack.enter_context(tc.tile_pool(name="codes", bufs=3 * ROUND_TILES))
+        vip_pool = stack.enter_context(
+            tc.tile_pool(name="vip", bufs=(X_LAG + 3) * ROUND_TILES)
+        )
+        som_pool = stack.enter_context(tc.tile_pool(name="som", bufs=4))
+        out_pool = stack.enter_context(tc.tile_pool(name="result", bufs=3))
+        psum = stack.enter_context(tc.psum_pool(name="psum", bufs=8))
+        stack.enter_context(tc.manual_schedule())
+
+        ident = const.tile([P, P], F32)
+        make_identity(nc, ident[:])
+
+        def as_pairs(words):
+            return words.rearrange("p (g b u) -> p g b u", g=D_PASSES, u=2)
+
+        def flip(words, dest, copy_out):
+            bank = psum.tile([P, BANK], F32, tag="bank")
+            for c in range(BLOCKS):
+                cols = slice(c * P, (c + 1) * P)
+                nc.tensor.transpose(bank[:, cols], words[:, cols], ident[:])
+            copy_out(out=dest, in_=bank[:].rearrange("p (g u b) -> p g b u", g=D_PASSES, u=2))
+
+        def quantise(grouped, codes, scales):
+            nc.vector.quantize_mx(out=codes.bitcast(FP8X4), scales=scales, in_=grouped)
+
+        def mx(acc, stationary, s_cols, moving, m_cols, start, stop):
+            nc.tensor.matmul_mx(
+                out=acc,
+                lhsT=stationary[0][:, s_cols].bitcast(FP8X4),
+                lhsT_scale=stationary[1][:, s_cols],
+                rhs=moving[0][:, m_cols].bitcast(FP8X4),
+                rhs_scale=moving[1][:, m_cols],
+                start=start,
+                stop=stop,
+            )
+
+        td_raw = const.tile([P, PACK * D_IN], BF16)
+        td_q = (
+            const.tile([P, PACK * D_PASSES * P], U32, name="td_codes", align_bytes=64),
+            const.tile([P, PACK * D_PASSES * P], U8, name="td_scales", align_bytes=64),
+        )
+        som_raw = const.tile([P, BLOCKS * D_IN], BF16)
+        som_grouped = const.tile([P, D_PASSES * CELLS * PACK], BF16, align_bytes=64)
+        som_q = (
+            const.tile([P, D_PASSES * CELLS], U32, name="som_codes", align_bytes=64),
+            const.tile([P, D_PASSES * CELLS], U8, name="som_scales", align_bytes=64),
+        )
+        vs_raw = const.tile([P, BLOCKS * CELLS], BF16)
+        vs_grouped = const.tile([P, CELLS * PACK], BF16, align_bytes=64)
+        vs_q = (
+            const.tile([P, CELLS], U32, name="vs_codes", align_bytes=64),
+            const.tile([P, CELLS], U8, name="vs_scales", align_bytes=64),
+        )
+
+        def either_copy(n):
+            return nc.scalar.copy if n % 2 == 0 else nc.vector.tensor_copy
+
+        def load_td():
+            rows = W_vip_td.rearrange("(u q e) k -> u q (e k)", u=2, e=2)
+            for u in range(2):
+                nc.sync.dma_start(out=td_raw[:, u * 2 * D_IN : (u + 1) * 2 * D_IN], in_=rows[u])
+
+        def prepare_td():
+            tiles = []
+            for j in range(PACK):
+                grouped = grouped_pool.tile([P, 2 * BANK], BF16, tag="grouped", align_bytes=64)
+                flip(
+                    td_raw[:].bitcast(F32)[:, j * BANK : (j + 1) * BANK],
+                    as_pairs(grouped[:].bitcast(F32)),
+                    either_copy(j),
+                )
+                tiles.append(grouped)
+            for j in range(PACK):
+                cols = slice(j * D_PASSES * P, (j + 1) * D_PASSES * P)
+                quantise(tiles[j][:], td_q[0][:, cols], td_q[1][:, cols])
+
+        def load_som_and_vs():
+            nc.sync.dma_start(
+                out=som_raw[:].rearrange("q (r k) -> q r k", r=BLOCKS),
+                in_=W_som_in.rearrange("(r q) k -> q r k", q=P),
+            )
+            nc.sync.dma_start(
+                out=vs_raw[:].rearrange("q (r k) -> q r k", r=BLOCKS),
+                in_=W_vip_som.rearrange("(r q) k -> q r k", q=P),
+            )
+
+        def prepare_som_and_vs():
+            som_words = som_grouped[:].bitcast(F32).rearrange(
+                "p (g r q u) -> p r g q u", g=D_PASSES, r=BLOCKS, u=2
+            )
+            for r in range(BLOCKS):
+                flip(
+                    som_raw[:].bitcast(F32)[:, r * BANK : (r + 1) * BANK],
+                    som_words[:, r],
+                    either_copy(r),
+                )
+            for h in range(2):
+                half = slice(h * BANK, (h + 1) * BANK)
+                flip(
+                    vs_raw[:].bitcast(F32)[:, half],
+                    as_pairs(vs_grouped[:].bitcast(F32)[:, half]),
+                    either_copy(h),
+                )
+            quantise(som_grouped[:], som_q[0][:], som_q[1][:])
+            quantise(vs_grouped[:], vs_q[0][:], vs_q[1][:])
+
+        raw = {}
+        grouped_of = {}
+        quantised = {}
+
+        def chunks_of(unit):
+            if 0 <= unit < UNITS:
+                return range(unit * ROUND_CHUNKS, (unit + 1) * ROUND_CHUNKS)
+            return range(0)
+
+        def tiles_of(unit):
+            return [c * CHUNK_TILES + t for c in chunks_of(unit) for t in range(CHUNK_TILES)]
+
+        def load(name, chunks, c):
+            rows = raw_pool.tile([P, CHUNK_TILES * D_IN], BF16, tag=name + "_raw")
+            nc.sync.dma_start(out=rows[:], in_=chunks[c])
+            raw[(name, c)] = rows
+
+        def loads_for_round(r):
+            if r == X_LAG + 1:
+                load_som_and_vs()
+            for c in chunks_of(r):
+                load("pred", pred_chunks, c)
+            for c in chunks_of(r - 1 - X_LAG):
+                load("x", x_chunks, c)
+
+        def flip_tile(name, i, copy_out):
+            c, t = divmod(i, CHUNK_TILES)
+            grouped = grouped_pool.tile([P, 2 * BANK], BF16, tag="grouped", align_bytes=64)
+            flip(
+                raw[(name, c)][:].bitcast(F32)[:, t * BANK : (t + 1) * BANK],
+                as_pairs(grouped[:].bitcast(F32)),
+                copy_out,
+            )
+            grouped_of[(name, i)] = grouped
+
+        def quantise_tile(name, i, pool):
+            grouped = grouped_of[(name, i)]
+            width = grouped.shape[1] // PACK
+            codes = pool.tile([P, width], U32, tag=name + "_codes", align_bytes=64)
+            scales = pool.tile([P, width], U8, tag=name + "_scales", align_bytes=64)
+            quantise(grouped[:], codes[:], scales[:])
+            quantised[(name, i)] = (codes, scales)
+
+        def vip_matmul(i):
+            bank = psum.tile([P, BANK], F32, tag="bank")
+            for j in range(PACK):
+                for g in range(D_PASSES):
+                    mx(
+                        bank[:, j * P : (j + 1) * P],
+                        td_q,
+                        slice((j * D_PASSES + g) * P, (j * D_PASSES + g + 1) * P),
+                        quantised[("pred", i)],
+                        slice(g * P, (g + 1) * P),
+                        start=(g == 0),
+                        stop=(g == D_PASSES - 1),
+                    )
+            vip = grouped_pool.tile([P, BANK], BF16, tag="vip", align_bytes=64)
+            nc.scalar.activation(
+                out=vip[:].rearrange("p (b j) -> p b j", j=PACK),
+                in_=bank[:].rearrange("p (j b) -> p b j", j=PACK),
+                func=RELU,
+            )
+            grouped_of[("vip", i)] = vip
+
+        def som_matmuls(i, result):
+            feed = psum.tile([P, BANK], F32, tag="bank")
+            for g in range(D_PASSES):
+                mx(
+                    feed[:],
+                    quantised[("x", i)],
+                    slice(g * P, (g + 1) * P),
+                    som_q,
+                    slice(g * CELLS, (g + 1) * CELLS),
+                    start=(g == 0),
+                    stop=(g == D_PASSES - 1),
+                )
+            som_ff = som_pool.tile([P, CELLS], F32)
+            nc.scalar.activation(out=som_ff[:], in_=feed[:], func=RELU)
+            inhibition = psum.tile([P, BANK], F32, tag="bank")
+            mx(
+                inhibition[:],
+                quantised[("vip", i)],
+                slice(0, P),
+                vs_q,
+                slice(0, CELLS),
+                start=True,
+                stop=True,
+            )
+            nc.vector.tensor_tensor(out=result, in0=som_ff[:], in1=inhibition[:], op=SUBTRACT)
+
+        load_td()
+        for r in range(LOAD_AHEAD):
+            loads_for_round(r)
+        prepare_td()
+
+        for r in range(UNITS + X_LAG + 2):
+            loads_for_round(r + LOAD_AHEAD)
+            if r == X_LAG + 1:
+                prepare_som_and_vs()
+
+            for i in tiles_of(r):
+                flip_tile("pred", i, nc.scalar.copy)
+            for i in tiles_of(r - 1 - X_LAG):
+                by_vector = i % VECTOR_SHARE == VECTOR_SHARE - 1
+                flip_tile("x", i, nc.vector.tensor_copy if by_vector else nc.scalar.copy)
+            for i in tiles_of(r):
+                quantise_tile("pred", i, codes_pool)
+            for i in tiles_of(r - 1 - X_LAG):
+                quantise_tile("x", i, codes_pool)
+
+            for i in tiles_of(r - 1):
+                vip_matmul(i)
+            for i in tiles_of(r - 1):
+                quantise_tile("vip", i, vip_pool)
+            for c in chunks_of(r - 2 - X_LAG):
+                result = out_pool.tile([P, CHUNK_TILES * CELLS], F32)
+                for t in range(CHUNK_TILES):
+                    som_matmuls(c * CHUNK_TILES + t, result[:, t * CELLS : (t + 1) * CELLS])
+                nc.vector.tensor_scalar_max(out=result[:], in0=result[:], scalar1=0.0)
+                nc.sync.dma_start(out=out_chunks[c], in_=result[:])

@@ -10,6 +10,8 @@ U8 = mybir.dt.uint8
 FP8X4 = mybir.dt.float8_e4m3fn_x4
 RELU = mybir.ActivationFunctionType.Relu
 SUBTRACT = mybir.AluOpType.subtract
+MIN = mybir.AluOpType.min
+MAX = mybir.AluOpType.max
 
 BATCH = 4096
 D_IN = 1024
@@ -26,12 +28,12 @@ BLOCKS = BANK // P
 TILES = BATCH // P
 CHUNK_TILES = 2
 CHUNKS = TILES // CHUNK_TILES
-ROUND_CHUNKS = 1
+ROUND_CHUNKS = 2
 ROUND_TILES = ROUND_CHUNKS * CHUNK_TILES
 UNITS = CHUNKS // ROUND_CHUNKS
-X_LAG = 2
-LOAD_AHEAD = 3
-VECTOR_SHARE = 4
+X_LAG = 1
+LOAD_AHEAD = 2
+VECTOR_SHARE = 2
 
 
 def tile_pecircuits_pa_t_kernel(
@@ -48,13 +50,13 @@ def tile_pecircuits_pa_t_kernel(
         raw_pool = stack.enter_context(
             tc.tile_pool(name="raw", bufs=(LOAD_AHEAD + 1) * ROUND_CHUNKS)
         )
-        grouped_pool = stack.enter_context(tc.tile_pool(name="grouped", bufs=4 * ROUND_TILES))
+        grouped_pool = stack.enter_context(tc.tile_pool(name="grouped", bufs=3 * ROUND_TILES))
         codes_pool = stack.enter_context(tc.tile_pool(name="codes", bufs=3 * ROUND_TILES))
         vip_pool = stack.enter_context(
             tc.tile_pool(name="vip", bufs=(X_LAG + 3) * ROUND_TILES)
         )
         som_pool = stack.enter_context(tc.tile_pool(name="som", bufs=4))
-        out_pool = stack.enter_context(tc.tile_pool(name="result", bufs=3))
+        out_pool = stack.enter_context(tc.tile_pool(name="result", bufs=6))
         psum = stack.enter_context(tc.psum_pool(name="psum", bufs=8))
         stack.enter_context(tc.manual_schedule())
 
@@ -219,7 +221,7 @@ def tile_pecircuits_pa_t_kernel(
             )
             grouped_of[("vip", i)] = vip
 
-        def som_matmuls(i, result):
+        def som_matmuls(i):
             feed = psum.tile([P, BANK], F32, tag="bank")
             for g in range(D_PASSES):
                 mx(
@@ -243,7 +245,13 @@ def tile_pecircuits_pa_t_kernel(
                 start=True,
                 stop=True,
             )
-            nc.vector.tensor_tensor(out=result, in0=som_ff[:], in1=inhibition[:], op=SUBTRACT)
+            result = out_pool.tile([P, CELLS], F32)
+            nc.vector.tensor_tensor(out=result[:], in0=som_ff[:], in1=inhibition[:], op=SUBTRACT)
+            nc.gpsimd.tensor_scalar(
+                out=result[:], in0=result[:], scalar1=float("inf"), scalar2=0.0, op0=MIN, op1=MAX
+            )
+            c, t = divmod(i, CHUNK_TILES)
+            nc.sync.dma_start(out=out_chunks[c][:, t * CELLS : (t + 1) * CELLS], in_=result[:])
 
         load_td()
         for r in range(LOAD_AHEAD):
@@ -269,9 +277,5 @@ def tile_pecircuits_pa_t_kernel(
                 vip_matmul(i)
             for i in tiles_of(r - 1):
                 quantise_tile("vip", i, vip_pool)
-            for c in chunks_of(r - 2 - X_LAG):
-                result = out_pool.tile([P, CHUNK_TILES * CELLS], F32)
-                for t in range(CHUNK_TILES):
-                    som_matmuls(c * CHUNK_TILES + t, result[:, t * CELLS : (t + 1) * CELLS])
-                nc.vector.tensor_scalar_max(out=result[:], in0=result[:], scalar1=0.0)
-                nc.sync.dma_start(out=out_chunks[c], in_=result[:])
+            for i in tiles_of(r - 2 - X_LAG):
+                som_matmuls(i)

@@ -10,8 +10,6 @@ U8 = mybir.dt.uint8
 FP8X4 = mybir.dt.float8_e4m3fn_x4
 RELU = mybir.ActivationFunctionType.Relu
 SUBTRACT = mybir.AluOpType.subtract
-MIN = mybir.AluOpType.min
-MAX = mybir.AluOpType.max
 
 BATCH = 4096
 D_IN = 1024
@@ -247,9 +245,7 @@ def tile_pecircuits_pa_t_kernel(
             )
             result = out_pool.tile([P, CELLS], F32)
             nc.vector.tensor_tensor(out=result[:], in0=som_ff[:], in1=inhibition[:], op=SUBTRACT)
-            nc.gpsimd.tensor_scalar(
-                out=result[:], in0=result[:], scalar1=float("inf"), scalar2=0.0, op0=MIN, op1=MAX
-            )
+            nc.vector.tensor_scalar_max(out=result[:], in0=result[:], scalar1=0.0)
             c, t = divmod(i, CHUNK_TILES)
             nc.sync.dma_start(out=out_chunks[c][:, t * CELLS : (t + 1) * CELLS], in_=result[:])
 

from contextlib import ExitStack

import concourse.mybir as mybir
from concourse.masks import make_identity

F32 = mybir.dt.float32
BF16 = mybir.dt.bfloat16
U32 = mybir.dt.uint32
U8 = mybir.dt.uint8
FP8X4 = mybir.dt.float8_e4m3fn_x4
RELU = mybir.ActivationFunctionType.Relu
SUBTRACT = mybir.AluOpType.subtract

BATCH = 4096
D_IN = 1024
CELLS = 512
FLOPS = 2 * BATCH * CELLS * (2 * D_IN + CELLS)

P = 128
PACK = 4
K_PASS = P * PACK
D_PASSES = D_IN // K_PASS
BANK = 512
BLOCKS = BANK // P

TILES = BATCH // P
CHUNK_TILES = 2
CHUNKS = TILES // CHUNK_TILES
ROUND_CHUNKS = 2
ROUND_TILES = ROUND_CHUNKS * CHUNK_TILES
UNITS = CHUNKS // ROUND_CHUNKS
X_LAG = 1
LOAD_AHEAD = 2
VECTOR_SHARE = 2


def tile_pecircuits_pa_t_kernel(
    tc, x_batch, predicted, W_vip_td, W_som_in, W_vip_som, out
):
    nc = tc.nc

    pred_chunks = predicted.rearrange("(c p t) k -> c p (t k)", p=P, t=CHUNK_TILES)
    x_chunks = x_batch.rearrange("(c p t) k -> c p (t k)", p=P, t=CHUNK_TILES)
    out_chunks = out.rearrange("(c p t) n -> c p (t n)", p=P, t=CHUNK_TILES)

    with ExitStack() as stack:
        const = stack.enter_context(tc.tile_pool(name="const", bufs=1))
        raw_pool = stack.enter_context(
            tc.tile_pool(name="raw", bufs=(LOAD_AHEAD + 1) * ROUND_CHUNKS)
        )
        grouped_pool = stack.enter_context(tc.tile_pool(name="grouped", bufs=3 * ROUND_TILES))
        codes_pool = stack.enter_context(tc.tile_pool(name="codes", bufs=3 * ROUND_TILES))
        vip_pool = stack.enter_context(
            tc.tile_pool(name="vip", bufs=(X_LAG + 3) * ROUND_TILES)
        )
        som_pool = stack.enter_context(tc.tile_pool(name="som", bufs=4))
        out_pool = stack.enter_context(tc.tile_pool(name="result", bufs=6))
        psum = stack.enter_context(tc.psum_pool(name="psum", bufs=8))
        stack.enter_context(tc.manual_schedule())

        ident = const.tile([P, P], F32)
        make_identity(nc, ident[:])

        def as_pairs(words):
            return words.rearrange("p (g b u) -> p g b u", g=D_PASSES, u=2)

        def flip(words, dest, copy_out):
            bank = psum.tile([P, BANK], F32, tag="bank")
            for c in range(BLOCKS):
                cols = slice(c * P, (c + 1) * P)
                nc.tensor.transpose(bank[:, cols], words[:, cols], ident[:])
            copy_out(out=dest, in_=bank[:].rearrange("p (g u b) -> p g b u", g=D_PASSES, u=2))

        def quantise(grouped, codes, scales):
            nc.vector.quantize_mx(out=codes.bitcast(FP8X4), scales=scales, in_=grouped)

        def mx(acc, stationary, s_cols, moving, m_cols, start, stop):
            nc.tensor.matmul_mx(
                out=acc,
                lhsT=stationary[0][:, s_cols].bitcast(FP8X4),
                lhsT_scale=stationary[1][:, s_cols],
                rhs=moving[0][:, m_cols].bitcast(FP8X4),
                rhs_scale=moving[1][:, m_cols],
                start=start,
                stop=stop,
            )

        td_raw = const.tile([P, PACK * D_IN], BF16)
        td_q = (
            const.tile([P, PACK * D_PASSES * P], U32, name="td_codes", align_bytes=64),
            const.tile([P, PACK * D_PASSES * P], U8, name="td_scales", align_bytes=64),
        )
        som_raw = const.tile([P, BLOCKS * D_IN], BF16)
        som_grouped = const.tile([P, D_PASSES * CELLS * PACK], BF16, align_bytes=64)
        som_q = (
            const.tile([P, D_PASSES * CELLS], U32, name="som_codes", align_bytes=64),
            const.tile([P, D_PASSES * CELLS], U8, name="som_scales", align_bytes=64),
        )
        vs_raw = const.tile([P, BLOCKS * CELLS], BF16)
        vs_grouped = const.tile([P, CELLS * PACK], BF16, align_bytes=64)
        vs_q = (
            const.tile([P, CELLS], U32, name="vs_codes", align_bytes=64),
            const.tile([P, CELLS], U8, name="vs_scales", align_bytes=64),
        )

        def either_copy(n):
            return nc.scalar.copy if n % 2 == 0 else nc.vector.tensor_copy

        def load_td():
            rows = W_vip_td.rearrange("(u q e) k -> u q (e k)", u=2, e=2)
            for u in range(2):
                nc.sync.dma_start(out=td_raw[:, u * 2 * D_IN : (u + 1) * 2 * D_IN], in_=rows[u])

        def prepare_td():
            tiles = []
            for j in range(PACK):
                grouped = grouped_pool.tile([P, 2 * BANK], BF16, tag="grouped", align_bytes=64)
                flip(
                    td_raw[:].bitcast(F32)[:, j * BANK : (j + 1) * BANK],
                    as_pairs(grouped[:].bitcast(F32)),
                    either_copy(j),
                )
                tiles.append(grouped)
            for j in range(PACK):
                cols = slice(j * D_PASSES * P, (j + 1) * D_PASSES * P)
                quantise(tiles[j][:], td_q[0][:, cols], td_q[1][:, cols])

        def load_som_and_vs():
            nc.sync.dma_start(
                out=som_raw[:].rearrange("q (r k) -> q r k", r=BLOCKS),
                in_=W_som_in.rearrange("(r q) k -> q r k", q=P),
            )
            nc.sync.dma_start(
                out=vs_raw[:].rearrange("q (r k) -> q r k", r=BLOCKS),
                in_=W_vip_som.rearrange("(r q) k -> q r k", q=P),
            )

        def prepare_som_and_vs():
            som_words = som_grouped[:].bitcast(F32).rearrange(
                "p (g r q u) -> p r g q u", g=D_PASSES, r=BLOCKS, u=2
            )
            for r in range(BLOCKS):
                flip(
                    som_raw[:].bitcast(F32)[:, r * BANK : (r + 1) * BANK],
                    som_words[:, r],
                    either_copy(r),
                )
            for h in range(2):
                half = slice(h * BANK, (h + 1) * BANK)
                flip(
                    vs_raw[:].bitcast(F32)[:, half],
                    as_pairs(vs_grouped[:].bitcast(F32)[:, half]),
                    either_copy(h),
                )
            quantise(som_grouped[:], som_q[0][:], som_q[1][:])
            quantise(vs_grouped[:], vs_q[0][:], vs_q[1][:])

        raw = {}
        grouped_of = {}
        quantised = {}

        def chunks_of(unit):
            if 0 <= unit < UNITS:
                return range(unit * ROUND_CHUNKS, (unit + 1) * ROUND_CHUNKS)
            return range(0)

        def tiles_of(unit):
            return [c * CHUNK_TILES + t for c in chunks_of(unit) for t in range(CHUNK_TILES)]

        def load(name, chunks, c):
            rows = raw_pool.tile([P, CHUNK_TILES * D_IN], BF16, tag=name + "_raw")
            nc.sync.dma_start(out=rows[:], in_=chunks[c])
            raw[(name, c)] = rows

        def loads_for_round(r):
            if r == X_LAG + 1:
                load_som_and_vs()
            for c in chunks_of(r):
                load("pred", pred_chunks, c)
            for c in chunks_of(r - 1 - X_LAG):
                load("x", x_chunks, c)

        def flip_tile(name, i, copy_out):
            c, t = divmod(i, CHUNK_TILES)
            grouped = grouped_pool.tile([P, 2 * BANK], BF16, tag="grouped", align_bytes=64)
            flip(
                raw[(name, c)][:].bitcast(F32)[:, t * BANK : (t + 1) * BANK],
                as_pairs(grouped[:].bitcast(F32)),
                copy_out,
            )
            grouped_of[(name, i)] = grouped

        def quantise_tile(name, i, pool):
            grouped = grouped_of[(name, i)]
            width = grouped.shape[1] // PACK
            codes = pool.tile([P, width], U32, tag=name + "_codes", align_bytes=64)
            scales = pool.tile([P, width], U8, tag=name + "_scales", align_bytes=64)
            quantise(grouped[:], codes[:], scales[:])
            quantised[(name, i)] = (codes, scales)

        def vip_matmul(i):
            bank = psum.tile([P, BANK], F32, tag="bank")
            for j in range(PACK):
                for g in range(D_PASSES):
                    mx(
                        bank[:, j * P : (j + 1) * P],
                        td_q,
                        slice((j * D_PASSES + g) * P, (j * D_PASSES + g + 1) * P),
                        quantised[("pred", i)],
                        slice(g * P, (g + 1) * P),
                        start=(g == 0),
                        stop=(g == D_PASSES - 1),
                    )
            vip = grouped_pool.tile([P, BANK], BF16, tag="vip", align_bytes=64)
            nc.scalar.activation(
                out=vip[:].rearrange("p (b j) -> p b j", j=PACK),
                in_=bank[:].rearrange("p (j b) -> p b j", j=PACK),
                func=RELU,
            )
            grouped_of[("vip", i)] = vip

        def som_matmuls(i):
            feed = psum.tile([P, BANK], F32, tag="bank")
            for g in range(D_PASSES):
                mx(
                    feed[:],
                    quantised[("x", i)],
                    slice(g * P, (g + 1) * P),
                    som_q,
                    slice(g * CELLS, (g + 1) * CELLS),
                    start=(g == 0),
                    stop=(g == D_PASSES - 1),
                )
            som_ff = som_pool.tile([P, CELLS], F32)
            nc.scalar.activation(out=som_ff[:], in_=feed[:], func=RELU)
            inhibition = psum.tile([P, BANK], F32, tag="bank")
            mx(
                inhibition[:],
                quantised[("vip", i)],
                slice(0, P),
                vs_q,
                slice(0, CELLS),
                start=True,
                stop=True,
            )
            result = out_pool.tile([P, CELLS], F32)
            nc.vector.tensor_tensor(out=result[:], in0=som_ff[:], in1=inhibition[:], op=SUBTRACT)
            nc.vector.tensor_scalar_max(out=result[:], in0=result[:], scalar1=0.0)
            c, t = divmod(i, CHUNK_TILES)
            nc.sync.dma_start(out=out_chunks[c][:, t * CELLS : (t + 1) * CELLS], in_=result[:])

        load_td()
        for r in range(LOAD_AHEAD):
            loads_for_round(r)
        prepare_td()

        for r in range(UNITS + X_LAG + 2):
            loads_for_round(r + LOAD_AHEAD)
            if r == X_LAG + 1:
                prepare_som_and_vs()

            for i in tiles_of(r):
                flip_tile("pred", i, nc.scalar.copy)
            for i in tiles_of(r - 1 - X_LAG):
                by_vector = i % VECTOR_SHARE == VECTOR_SHARE - 1
                flip_tile("x", i, nc.vector.tensor_copy if by_vector else nc.scalar.copy)
            for i in tiles_of(r):
                quantise_tile("pred", i, codes_pool)
            for i in tiles_of(r - 1 - X_LAG):
                quantise_tile("x", i, codes_pool)

            for i in tiles_of(r - 1):
                vip_matmul(i)
            for i in tiles_of(r - 1):
                quantise_tile("vip", i, vip_pool)
            for i in tiles_of(r - 2 - X_LAG):
                som_matmuls(i)
